import numpy as np
import ml_dtypes


def mxq(x, axis, fmt="e4m3"):
    dtype, down = {"e4m3": (ml_dtypes.float8_e4m3fn, 7), "e5m2": (ml_dtypes.float8_e5m2, 14)}[fmt]
    v = np.moveaxis(np.asarray(x, np.float32).astype(ml_dtypes.bfloat16).astype(np.float64), axis, -1)
    blocks = v.reshape(v.shape[:-1] + (-1, 32))
    amax = np.abs(blocks).max(-1, keepdims=True)
    byte = np.maximum(np.where(amax > 0, np.frexp(amax)[1] - 1 + 127, 0) - down, 1)
    scale = np.exp2(byte - 127.0)
    codes = (blocks / scale).astype(np.float32).astype(dtype).astype(np.float64)
    return np.moveaxis((codes * scale).reshape(v.shape), -1, axis)


WIDE = False


def mx_kscale(k):
    if not WIDE:
        return np.ones(k)
    levels = np.array([10, -10, 5, -5, 0])
    if k % 512:
        return np.exp2(np.random.permutation(np.resize(levels, k // 32))).repeat(32)
    a = np.empty((k // 512, 16))
    for p in range(k // 512):
        a[p, :8] = np.random.permutation(np.resize(levels, 8))
        for g in range(8):
            far = levels[np.abs(levels - a[p, g]) >= 10]
            a[p, g + 8] = far[np.random.randint(len(far))]
    return np.exp2(a.ravel()).repeat(32)


BF16 = ml_dtypes.bfloat16


def bf(x):
    return np.asarray(x, np.float32).astype(BF16)


def f64(x):
    return np.asarray(x).astype(np.float64)


B, K, N = 1024, 2048, 2048
EPS = 1e-5
GELU_C = 0.7978845608


def setup_inputs():
    s = mx_kscale(K)
    return {"x": bf(np.random.standard_normal((B, K)) * s),
            "weight": bf(np.random.standard_normal((K, N)) * np.sqrt(2.0 / K) / s[:, None]),
            "bn_gamma": bf(np.random.uniform(0.5, 1.5, N)),
            "bn_beta": bf(np.random.standard_normal(N) * 0.1),
            "bn_mean": bf(np.random.standard_normal(N) * 0.1),
            "bn_var": bf(np.random.uniform(0.5, 1.5, N))}


def core(x, weight, bn_gamma, bn_beta, bn_mean, bn_var):
    acc = mxq(f64(x), 1, "e4m3") @ mxq(f64(weight), 0, "e4m3")
    x_norm = (acc - f64(bn_mean)) / np.sqrt(f64(bn_var) + EPS)
    bn_out = f64(bn_gamma) * x_norm + f64(bn_beta)
    gelu = 0.5 * bn_out * (1.0 + np.tanh(GELU_C * (bn_out + 0.044715 * bn_out * bn_out * bn_out)))
    return np.maximum(gelu, 0.0)


def e4m3fn_bytes(y):
    return np.clip(np.asarray(y, np.float64), -448.0, 448.0).astype(np.float32).astype(ml_dtypes.float8_e4m3fn).view(np.uint8)


def reference(x, weight, bn_gamma, bn_beta, bn_mean, bn_var):
    out = core(x, weight, bn_gamma, bn_beta, bn_mean, bn_var)
    s = np.max(np.abs(out), axis=-1, keepdims=True) / 448.0
    return out, e4m3fn_bytes(out / s)

@@ -1,0 +1,434 @@
+from contextlib import ExitStack
+
+import concourse.mybir as mybir
+from concourse.masks import make_identity
+
+TOKENS, K, CHANNELS = 1024, 2048, 2048
+EPS = 1e-5
+FLOPS = 2 * TOKENS * K * CHANNELS
+
+F32 = mybir.dt.float32
+BF16 = mybir.dt.bfloat16
+U32 = mybir.dt.uint32
+U8 = mybir.dt.uint8
+FP8X4 = mybir.dt.float8_e4m3fn_x4
+FP8 = mybir.dt.float8_e4m3fn
+ACT = mybir.ActivationFunctionType
+ALU = mybir.AluOpType
+ENGINE = mybir.EngineType
+
+P = 128
+PASSES = range(4)
+CHANNEL_TILES = range(4)
+LAST_GROUP = 3
+
+STEPS = [
+    (0, 0, 4), (0, 4, 4), (1, 0, 4), (1, 4, 4), (2, 0, 4), (3, 0, 2),
+    (3, 2, 2), (2, 4, 2), (3, 4, 2), (2, 6, 2), (3, 6, 1), (3, 7, 1),
+]
+FIRST_STEP = 0
+OWN_BANK = (0, 10, 11)
+
+SLOTS = {"big": 4, "raw": 4, "x4": 8, "w4": 3, "acc": 4, "turn": 4, "gelu": 8, "fp8": 4}
+W_COLS_VECTOR = 288
+CAST_COLS_VECTOR = 1280
+
+VECTOR_HEAD = (
+    "xc.0.0 wv.0 xq.0.0 xq.1.0 xc.0.1 wq.0 xq.0.1 xq.1.1 wv.1 wq.1 xc.0.2 wv.2 xq.0.2 wq.2 xq.1.2 xc.0.3 wv.3 xq.0.3 xq.1.3 wq.3 "
+    "xc.2.0 xq.2.0 xq.3.0 xc.2.1 wv.4 xq.2.1 xc.2.2 xq.3.1 xq.2.2 xc.2.3 wq.4 xq.3.2 xq.2.3 xq.3.3"
+)
+SCALAR_HEAD = (
+    "xc.1.0 ws.0 xc.1.1 ws.1 bn ws.2 xc.1.2 ws.3 xc.1.3 xc.3.0 ge.0.0 ge.0.1 ge.0.2 ge.0.3 xc.3.1 ws.4 xc.3.2 xc.3.3 ws.5 ws.6 ws.7"
+)
+AFTER_GELU = {
+    (1, 2): "ws.8", (2, 0): "ws.9", (2, 2): "ws.10", (2, 3): "ws.11 ws.12", (3, 2): "ws.13", (3, 3): "ws.14 ws.15",
+    (7, 1): "cs.0 cs.1", (8, 1): "cs.2 cs.3", (10, 3): "cs.4 cs.5", (11, 3): "cs.6 cs.7",
+}
+FIRST_LATE_CHUNK = 5
+
+
+def parse_items(text):
+    return [(word.split(".")[0],) + tuple(int(number) for number in word.split(".")[1:]) for word in text.split()]
+
+
+def tiles_of(s):
+    return [STEPS[s][1] + i for i in range(STEPS[s][2])]
+
+
+def bank_of(s, c):
+    width = STEPS[s][2]
+    if s in OWN_BANK or width == 4:
+        return c, 0
+    return (c * width) // 4, ((c * width) % 4) * P
+
+
+def step_with(group, t):
+    s = [i for i in range(len(STEPS)) if STEPS[i][0] == group and t in tiles_of(i)][0]
+    return s, t - STEPS[s][1]
+
+
+def engine_orders():
+    per_tile = lambda kind, s: [(kind, s, i) for i in range(STEPS[s][2])]
+    steps = range(len(STEPS))
+
+    tensor = []
+    for run in range(8):
+        half, g = run // 4, run % 4
+        tensor += [("xt", 2 * half, g), ("xt", 2 * half + 1, g)]
+        if run == 1:
+            tensor += [("bt",)]
+        if 1 <= run <= 4:
+            tensor += [("mm", FIRST_STEP, run - 1)]
+    tensor += per_tile("ot", FIRST_STEP) + [("mm", 1, c) for c in CHANNEL_TILES]
+    for s in steps[2:]:
+        tensor += [("mm", s, c) for c in CHANNEL_TILES] + per_tile("ot", s - 1)
+    tensor += per_tile("ot", steps[-1])
+
+    vector = parse_items(VECTOR_HEAD)
+    finished = []
+    for s in steps:
+        trio = list(range(FIRST_LATE_CHUNK + 3 * s, min(FIRST_LATE_CHUNK + 3 * s + 3, 16)))
+        relus = per_tile("re", s)
+        vector += [("wv", n) for n in trio[:2]] + [("wq", n) for n in trio[:2]]
+        if len(trio) == 3:
+            vector += [("wv", trio[2]), relus[0], ("wq", trio[2])] + relus[1:]
+        else:
+            vector += relus
+        if STEPS[s][0] == LAST_GROUP:
+            finished += [s]
+            if tiles_of(s)[-1] % 2 == 1:
+                vector += [("sc", done) for done in finished] + [("cv", t) for done in finished for t in tiles_of(done)]
+                finished = []
+
+    scalar = parse_items(SCALAR_HEAD)
+    for s in steps[1:]:
+        for c in CHANNEL_TILES:
+            scalar += [("ge", s, c)] + parse_items(AFTER_GELU.get((s, c), ""))
+
+    queue = [("lx", 0, 0), ("lw", 0), ("lw", 1), ("lx", 0, 1), ("lw", 2), ("lw", 3), ("lx", 1, 0), ("lx", 1, 1)]
+    queue += [("lw", n) for n in range(4, 8)] + [("l2", g) for g in PASSES]
+    for s in steps:
+        if STEPS[s][0] % 2 == 1:
+            queue += per_tile("s0", s)
+        if STEPS[s][0] == LAST_GROUP:
+            queue += [("s1", t) for t in tiles_of(s)]
+    return [tensor, vector, scalar, queue]
+
+
+def tile_modelnew_kernel(tc, x, weight, bn_gamma, bn_beta, bn_mean, bn_var, out_0, out_1):
+    nc = tc.nc
+    with ExitStack() as ctx:
+        const = ctx.enter_context(tc.tile_pool(name="const", bufs=1))
+        keep = ctx.enter_context(tc.tile_pool(name="keep", bufs=1))
+        work = ctx.enter_context(tc.tile_pool(name="work", bufs=1))
+        psum = ctx.enter_context(tc.psum_pool(name="psum", bufs=4))
+        ctx.enter_context(tc.manual_schedule(engines={ENGINE.PE, ENGINE.DVE, ENGINE.Activation}))
+
+        ident = const.tile([P, P], F32, name="ident")
+        make_identity(nc, ident[:])
+        zero = const.tile([P, 1], F32, name="zero")
+        nc.gpsimd.memset(zero[:], 0.0)
+        neg_half = const.tile([P, 16], F32, name="neg_half")
+        nc.gpsimd.memset(neg_half[:], -0.5)
+        vec_bf = const.tile([P, P], BF16, name="vec_bf")
+        nc.gpsimd.memset(vec_bf[64:128, :], 0.0)
+        for v, vec in enumerate((bn_gamma, bn_beta, bn_mean, bn_var)):
+            nc.scalar.dma_start(out=vec_bf[16 * v : 16 * v + 16, :], in_=vec.rearrange("(i p) -> i p", p=P))
+        table_warmer = const.tile([P, 1], F32, name="table_warmer")
+        nc.scalar.activation(out=table_warmer[:], in_=zero[:], func=ACT.Gelu_apprx_tanh)
+        vec_f32 = const.tile([P, P], F32, name="vec_f32")
+        nc.gpsimd.tensor_copy(out=vec_f32[:], in_=vec_bf[:])
+        bn_cols = const.tile([P, 64], F32, name="bn_cols")
+        bn_tmp = const.tile([P, 3, 16], F32, name="bn_tmp")
+        bn_scale = const.tile([P, 16], F32, name="bn_scale")
+        bn_bias = const.tile([P, 16], F32, name="bn_bias")
+        row_max = const.tile([P, 8, 4], F32, name="row_max")
+        row_inv = const.tile([P, 8], F32, name="row_inv")
+        row_factor = const.tile([P, 8], F32, name="row_factor")
+
+        x_codes = [keep.tile([P, 4, 512], U32, name="x_codes%d" % half, align_bytes=64) for half in range(2)]
+        x_scales = [keep.tile([P, 4, 512], U8, name="x_scales%d" % half, align_bytes=64) for half in range(2)]
+        w_codes = [keep.tile([P, 4, 512], U32, name="w_codes%d" % group, align_bytes=64) for group in range(4)]
+        w_scales = [keep.tile([P, 4, 512], U8, name="w_scales%d" % group, align_bytes=64) for group in range(4)]
+        result = keep.tile([P, 8, CHANNELS], F32, name="result")
+
+        tiles = {}
+        history = {}
+        readers_left = {}
+
+        def has_room(tag, count):
+            have = history.setdefault(tag, [])
+            for extra in range(count):
+                old = len(have) + extra - SLOTS[tag]
+                if old >= 0 and (old >= len(have) or readers_left[(tag, have[old])] > 0):
+                    return False
+            return True
+
+        def new_tile(tag, key, readers, shape, dtype):
+            if tag in ("acc", "turn"):
+                fresh = psum.tile(shape, dtype, name=tag, tag=tag, bufs=SLOTS[tag])
+            else:
+                fresh = work.tile(shape, dtype, name=tag, tag=tag, bufs=SLOTS[tag], align_bytes=64)
+            tiles[(tag, key)] = fresh
+            history.setdefault(tag, []).append(key)
+            readers_left[(tag, key)] = readers
+            return fresh
+
+        def read(tag, key):
+            readers_left[(tag, key)] -= 1
+            return tiles[(tag, key)]
+
+        def raw_home(n):
+            if n < 4:
+                return "raw", n
+            if n < 8:
+                return "big", ("group 1", (n - 4) // 2)
+            return "big", ("groups 2 and 3", n % 4)
+
+        def needs(item):
+            kind = item[0]
+            if kind == "xt":
+                return [("lx", item[1] // 2, item[2] // 2)]
+            if kind == "xc":
+                return [("xt", item[1], item[2])]
+            if kind == "xq":
+                return [("xc", item[1], item[2])]
+            if kind in ("wv", "ws"):
+                return [("lw", item[1])] if item[1] < 8 else [("l2", item[1] % 4)]
+            if kind == "wq":
+                return [("wv", item[1]), ("ws", item[1])]
+            if kind == "bn":
+                return [("bt",)]
+            if kind == "mm":
+                s, part = item[1], item[2]
+                passes = [part] if s == FIRST_STEP else PASSES
+                pairs = sorted(set(t // 2 for t in tiles_of(s)))
+                return [("xq", pr, g) for pr in pairs for g in passes] + [("wq", 4 * STEPS[s][0] + g) for g in passes]
+            if kind == "ge":
+                s, c = item[1], item[2]
+                if s == FIRST_STEP:
+                    return [("mm", s, 3), ("bn",)]
+                return [("mm", s, cc) for cc in CHANNEL_TILES if bank_of(s, cc)[0] == bank_of(s, c)[0]] + [("bn",)]
+            if kind == "ot":
+                return [("ge", item[1], c) for c in CHANNEL_TILES]
+            if kind == "re":
+                return [("ot", item[1], item[2])]
+            if kind == "s0":
+                return [("re", item[1], item[2]), ("re",) + step_with(STEPS[item[1]][0] - 1, tiles_of(item[1])[item[2]])]
+            if kind == "sc":
+                return [("re", item[1], i) for i in range(STEPS[item[1]][2])]
+            if kind in ("cv", "cs"):
+                return [("sc", step_with(LAST_GROUP, item[1])[0])]
+            if kind == "s1":
+                return [("cv", item[1]), ("cs", item[1])]
+            return []
+
+        def new_tiles(item):
+            kind = item[0]
+            if kind in ("lx", "l2"):
+                return "big", 1
+            if kind == "lw":
+                return raw_home(item[1])[0], 0 if raw_home(item[1]) in tiles else 1
+            if kind in ("xt", "ot"):
+                return "turn", 1
+            if kind == "xc":
+                return "x4", 1
+            if kind in ("wv", "ws"):
+                return "w4", 0 if ("w4", item[1]) in tiles else 1
+            if kind == "bt":
+                return "acc", 1
+            if kind == "mm":
+                s, part = item[1], item[2]
+                if s == FIRST_STEP:
+                    return "acc", 4 if part == 0 else 0
+                return "acc", 0 if ("acc", (s, bank_of(s, part)[0])) in tiles else 1
+            if kind == "ge":
+                return "gelu", 1
+            if kind in ("cv", "cs"):
+                return "fp8", 0 if ("fp8", item[1]) in tiles else 1
+            return "", 0
+
+        def one_pass(s, c, g):
+            group, t0, width = STEPS[s]
+            half, col, cols = t0 // 4, (t0 % 4) * P, width * P
+            bank, first = bank_of(s, c)
+            channels = slice(c * P, (c + 1) * P)
+            nc.tensor.matmul_mx(
+                out=tiles[("acc", (s, bank))][:, first : first + cols],
+                lhsT=w_codes[group][:, g, channels].bitcast(FP8X4),
+                lhsT_scale=w_scales[group][:, g, channels],
+                rhs=x_codes[half][:, g, col : col + cols].bitcast(FP8X4),
+                rhs_scale=x_scales[half][:, g, col : col + cols],
+                start=(g == 0),
+                stop=(g == 3),
+            )
+
+        def interleave(n, copy, first, last):
+            if ("w4", n) not in tiles:
+                new_tile("w4", n, 1, [P, 512, 4], BF16)
+            tag, key = raw_home(n)
+            raw = read(tag, key)
+            if n < 4:
+                rows = raw[:, :, first:last]
+            elif n < 8:
+                rows = raw[:, n % 2, :, first:last]
+            else:
+                rows = raw[:, :, 512 * (n // 4 - 2) + first : 512 * (n // 4 - 2) + last]
+            copy(out=tiles[("w4", n)][:, first:last, :], in_=rows.rearrange("p j w -> p w j"))
+
+        def write_down(item):
+            kind = item[0]
+            if kind == "lx":
+                half, k_half = item[1], item[2]
+                dest = new_tile("big", (half, k_half), 4, [P, 4, 1024], BF16)
+                rows = x[512 * half : 512 * (half + 1), 1024 * k_half : 1024 * (k_half + 1)]
+                nc.sync.dma_start(out=dest[:], in_=rows.rearrange("(i p) k -> p i k", p=P))
+            elif kind == "lw":
+                n = item[1]
+                group, g = n // 4, n % 4
+                if n < 4:
+                    dest = new_tile("raw", n, 2, [P, 4, 512], BF16)[:]
+                else:
+                    if raw_home(n) not in tiles:
+                        new_tile("big", raw_home(n)[1], 4, [P, 2, 4, 512], BF16)
+                    dest = tiles[raw_home(n)][:, n % 2, :, :]
+                rows = weight[512 * g : 512 * (g + 1), 512 * group : 512 * (group + 1)]
+                nc.sync.dma_start(out=dest, in_=rows.rearrange("(p j) w -> p j w", j=4))
+            elif kind == "l2":
+                g = item[1]
+                dest = new_tile("big", ("groups 2 and 3", g), 4, [P, 4, 1024], BF16)
+                nc.sync.dma_start(out=dest[:], in_=weight[512 * g : 512 * (g + 1), 1024:2048].rearrange("(p j) w -> p j w", j=4))
+            elif kind == "xt":
+                pr, g = item[1], item[2]
+                bank = new_tile("turn", ("x", pr, g), 1, [P, 2, 2, P], F32)
+                loaded = read("big", (pr // 2, g // 2))
+                for i in range(2):
+                    words = loaded[:, 2 * (pr % 2) + i, 512 * (g % 2) : 512 * (g % 2 + 1)].bitcast(F32)
+                    for u in range(2):
+                        nc.tensor.transpose(bank[:, i, u, :], words[:, u:256:2], ident[:])
+            elif kind == "xc":
+                pr, g = item[1], item[2]
+                dest = new_tile("x4", (pr, g), 1, [P, 256, 4], BF16)
+                dst = dest[:].bitcast(F32).rearrange("p (i r) u -> p i r u", i=2)
+                src = read("turn", ("x", pr, g))[:].rearrange("p i u r -> p i r u")
+                if pr % 2 == 0:
+                    nc.vector.tensor_copy(out=dst, in_=src)
+                else:
+                    nc.scalar.copy(out=dst, in_=src)
+            elif kind == "xq":
+                pr, g = item[1], item[2]
+                half, col = pr // 2, (pr % 2) * 256
+                nc.vector.quantize_mx(
+                    out=x_codes[half][:, g, col : col + 256].bitcast(FP8X4),
+                    scales=x_scales[half][:, g, col : col + 256],
+                    in_=read("x4", (pr, g))[:].rearrange("p r j -> p (r j)"),
+                )
+            elif kind == "wv":
+                interleave(item[1], nc.vector.tensor_copy, 0, W_COLS_VECTOR)
+            elif kind == "ws":
+                interleave(item[1], nc.scalar.copy, W_COLS_VECTOR, 512)
+            elif kind == "wq":
+                group, g = item[1] // 4, item[1] % 4
+                nc.vector.quantize_mx(
+                    out=w_codes[group][:, g, :].bitcast(FP8X4),
+                    scales=w_scales[group][:, g, :],
+                    in_=read("w4", item[1])[:].rearrange("p w j -> p (w j)"),
+                )
+            elif kind == "bt":
+                bank = new_tile("acc", "bn", 1, [P, 512], F32)
+                nc.tensor.transpose(bank[:, 0:P], vec_f32[:], ident[:])
+            elif kind == "bn":
+                nc.scalar.copy(out=bn_cols[:], in_=read("acc", "bn")[:, 0:64])
+                gamma, beta, mean, var = [bn_cols[:, 16 * v : 16 * v + 16] for v in range(4)]
+                nc.gpsimd.tensor_scalar(out=bn_tmp[:, 0, :], in0=var, scalar1=EPS, scalar2=None, op0=ALU.add)
+                nc.gpsimd.tensor_tensor(out=bn_tmp[:, 1, :], in0=bn_tmp[:, 0, :], in1=neg_half[:], op=ALU.pow)
+                nc.gpsimd.tensor_tensor(out=bn_scale[:], in0=gamma, in1=bn_tmp[:, 1, :], op=ALU.mult)
+                nc.gpsimd.tensor_tensor(out=bn_tmp[:, 2, :], in0=mean, in1=bn_scale[:], op=ALU.mult)
+                nc.gpsimd.tensor_tensor(out=bn_bias[:], in0=beta, in1=bn_tmp[:, 2, :], op=ALU.subtract)
+            elif kind == "mm":
+                s, part = item[1], item[2]
+                banks = sorted(set(bank_of(s, c)[0] for c in CHANNEL_TILES))
+                for bank in banks:
+                    if ("acc", (s, bank)) not in tiles and (s == FIRST_STEP or bank == bank_of(s, part)[0]):
+                        new_tile("acc", (s, bank), 4 // len(banks), [P, 512], F32)
+                for other in range(4):
+                    if s == FIRST_STEP:
+                        one_pass(s, other, part)
+                    else:
+                        one_pass(s, part, other)
+            elif kind == "ge":
+                s, c = item[1], item[2]
+                cols = STEPS[s][2] * P
+                bank, first = bank_of(s, c)
+                tile_no = 4 * STEPS[s][0] + c
+                dest = new_tile("gelu", (s, c), STEPS[s][2], [P, cols], F32)
+                nc.scalar.activation(
+                    out=dest[:],
+                    in_=read("acc", (s, bank))[:, first : first + cols],
+                    func=ACT.Gelu_apprx_tanh,
+                    bias=bn_bias[:, tile_no : tile_no + 1],
+                    scale=bn_scale[:, tile_no : tile_no + 1],
+                )
+            elif kind == "ot":
+                s, i = item[1], item[2]
+                bank = new_tile("turn", ("out", s, i), 1, [P, 512], F32)
+                for c in CHANNEL_TILES:
+                    nc.tensor.transpose(bank[:, c * P : (c + 1) * P], read("gelu", (s, c))[:, i * P : (i + 1) * P], ident[:])
+            elif kind == "re":
+                s, i = item[1], item[2]
+                group, t = STEPS[s][0], tiles_of(s)[i]
+                nc.vector.tensor_scalar(
+                    out=result[:, t, 512 * group : 512 * (group + 1)],
+                    in0=read("turn", ("out", s, i))[:],
+                    scalar1=0.0,
+                    scalar2=(row_max[:, t, group - 1 : group] if group > 0 else None),
+                    op0=ALU.max,
+                    op1=ALU.max,
+                    accum_out=row_max[:, t, group : group + 1],
+                )
+            elif kind == "s0":
+                group, t = STEPS[item[1]][0], tiles_of(item[1])[item[2]]
+                cols = slice(512 * (group - 1), 512 * (group + 1))
+                nc.sync.dma_start(out=out_0[t * P : (t + 1) * P, cols], in_=result[:, t, cols])
+            elif kind == "sc":
+                ts = slice(tiles_of(item[1])[0], tiles_of(item[1])[-1] + 1)
+                nc.vector.reciprocal(out=row_inv[:, ts], in_=row_max[:, ts, LAST_GROUP])
+                nc.vector.tensor_scalar(out=row_factor[:, ts], in0=row_inv[:, ts], scalar1=448.0, scalar2=None, op0=ALU.mult)
+            elif kind in ("cv", "cs"):
+                t = item[1]
+                if ("fp8", t) not in tiles:
+                    new_tile("fp8", t, 1, [P, CHANNELS], FP8)
+                factor = row_factor[:, t : t + 1]
+                if kind == "cv":
+                    nc.vector.tensor_scalar(
+                        out=tiles[("fp8", t)][:, 0:CAST_COLS_VECTOR], in0=result[:, t, 0:CAST_COLS_VECTOR],
+                        scalar1=factor, scalar2=None, op0=ALU.mult, saturate=False,
+                    )
+                else:
+                    nc.scalar.activation(
+                        out=tiles[("fp8", t)][:, CAST_COLS_VECTOR:CHANNELS], in_=result[:, t, CAST_COLS_VECTOR:CHANNELS],
+                        func=ACT.Identity, bias=zero[:, 0:1], scale=factor, saturate=False,
+                    )
+            elif kind == "s1":
+                t = item[1]
+                nc.sync.dma_start(out=out_1[t * P : (t + 1) * P, :], in_=read("fp8", t)[:].bitcast(U8))
+
+        def merge_orders(orders):
+            written = set()
+            heads = [0 for order in orders]
+            moved = True
+            while moved:
+                moved = False
+                for e in range(len(orders)):
+                    while heads[e] < len(orders[e]):
+                        item = orders[e][heads[e]]
+                        tag, count = new_tiles(item)
+                        if not all(need in written for need in needs(item)) or (count > 0 and not has_room(tag, count)):
+                            break
+                        write_down(item)
+                        written.add(item)
+                        heads[e] += 1
+                        moved = True
+            assert all(heads[e] == len(orders[e]) for e in range(len(orders))), "the orders block each other"
+
+        merge_orders(engine_orders())

@@ -44,6 +44,7 @@ AFTER_GELU = {
     (1, 2): "ws.8", (2, 0): "ws.9", (2, 2): "ws.10", (2, 3): "ws.11 ws.12", (3, 2): "ws.13", (3, 3): "ws.14 ws.15",
     (7, 1): "cs.0 cs.1", (8, 1): "cs.2 cs.3", (10, 3): "cs.4 cs.5", (11, 3): "cs.6 cs.7",
 }
+CLOCK_KEEPERS = {("xt", 2, 2): 2, ("ot", 0, 0): 2}
 FIRST_LATE_CHUNK = 5
 
 
@@ -126,6 +127,8 @@ def tile_modelnew_kernel(tc, x, weight, bn_gamma, bn_beta, bn_mean, bn_var, out_
 
         ident = const.tile([P, P], F32, name="ident")
         make_identity(nc, ident[:])
+        warm = const.tile([P, 512], BF16, name="warm")
+        nc.gpsimd.memset(warm[:], 0.0)
         zero = const.tile([P, 1], F32, name="zero")
         nc.gpsimd.memset(zero[:], 0.0)
         neg_half = const.tile([P, 16], F32, name="neg_half")
@@ -301,6 +304,8 @@ def tile_modelnew_kernel(tc, x, weight, bn_gamma, bn_beta, bn_mean, bn_var, out_
             elif kind == "xt":
                 pr, g = item[1], item[2]
                 bank = new_tile("turn", ("x", pr, g), 1, [P, 2, 2, P], F32)
+                for d in range(CLOCK_KEEPERS.get(item, 0)):
+                    nc.tensor.matmul(out=bank[:].rearrange("p i u r -> p (i u r)"), lhsT=warm[:, 0:P], rhs=warm[:], start=True, stop=True)
                 loaded = read("big", (pr // 2, g // 2))
                 for i in range(2):
                     words = loaded[:, 2 * (pr % 2) + i, 512 * (g % 2) : 512 * (g % 2 + 1)].bitcast(F32)
@@ -372,6 +377,8 @@ def tile_modelnew_kernel(tc, x, weight, bn_gamma, bn_beta, bn_mean, bn_var, out_
             elif kind == "ot":
                 s, i = item[1], item[2]
                 bank = new_tile("turn", ("out", s, i), 1, [P, 512], F32)
+                for d in range(CLOCK_KEEPERS.get(item, 0)):
+                    nc.tensor.matmul(out=bank[:], lhsT=warm[:, 0:P], rhs=warm[:], start=True, stop=True)
                 for c in CHANNEL_TILES:
                     nc.tensor.transpose(bank[:, c * P : (c + 1) * P], read("gelu", (s, c))[:, i * P : (i + 1) * P], ident[:])
             elif kind == "re":

@@ -34,7 +34,7 @@ W_COLS_VECTOR = 288
 CAST_COLS_VECTOR = 1280
 
 VECTOR_HEAD = (
-    "xc.0.0 wv.0 xq.0.0 xq.1.0 xc.0.1 wq.0 xq.0.1 xq.1.1 wv.1 wq.1 xc.0.2 wv.2 xq.0.2 wq.2 xq.1.2 xc.0.3 wv.3 xq.0.3 xq.1.3 wq.3 "
+    "xc.0.0 xc.0.1 xq.0.0 wv.0 xq.1.0 wq.0 xq.0.1 xq.1.1 wv.1 wq.1 xc.0.2 wv.2 xq.0.2 wq.2 xq.1.2 xc.0.3 wv.3 xq.0.3 xq.1.3 wq.3 "
     "xc.2.0 xq.2.0 xq.3.0 xc.2.1 wv.4 xq.2.1 xc.2.2 xq.3.1 xq.2.2 xc.2.3 wq.4 xq.3.2 xq.2.3 xq.3.3"
 )
 SCALAR_HEAD = (
@@ -44,6 +44,7 @@ AFTER_GELU = {
     (1, 2): "ws.8", (2, 0): "ws.9", (2, 2): "ws.10", (2, 3): "ws.11 ws.12", (3, 2): "ws.13", (3, 3): "ws.14 ws.15",
     (7, 1): "cs.0 cs.1", (8, 1): "cs.2 cs.3", (10, 3): "cs.4 cs.5", (11, 3): "cs.6 cs.7",
 }
+FIRST_LOAD_PIECES = 2
 CLOCK_KEEPERS = {("xt", 2, 2): 2, ("ot", 0, 0): 2}
 FIRST_LATE_CHUNK = 5
 
@@ -72,13 +73,11 @@ def engine_orders():
     per_tile = lambda kind, s: [(kind, s, i) for i in range(STEPS[s][2])]
     steps = range(len(STEPS))
 
-    tensor = []
-    for run in range(8):
+    tensor = [("xt", 0, 0), ("xt", 0, 1), ("xt", 1, 0), ("xt", 1, 1), ("bt",), ("mm", FIRST_STEP, 0)]
+    for run in range(2, 8):
         half, g = run // 4, run % 4
         tensor += [("xt", 2 * half, g), ("xt", 2 * half + 1, g)]
-        if run == 1:
-            tensor += [("bt",)]
-        if 1 <= run <= 4:
+        if run <= 4:
             tensor += [("mm", FIRST_STEP, run - 1)]
     tensor += per_tile("ot", FIRST_STEP) + [("mm", 1, c) for c in CHANNEL_TILES]
     for s in steps[2:]:
@@ -284,8 +283,14 @@ def tile_modelnew_kernel(tc, x, weight, bn_gamma, bn_beta, bn_mean, bn_var, out_
             if kind == "lx":
                 half, k_half = item[1], item[2]
                 dest = new_tile("big", (half, k_half), 4, [P, 4, 1024], BF16)
-                rows = x[512 * half : 512 * (half + 1), 1024 * k_half : 1024 * (k_half + 1)]
-                nc.sync.dma_start(out=dest[:], in_=rows.rearrange("(i p) k -> p i k", p=P))
+                pieces = FIRST_LOAD_PIECES if (half, k_half) == (0, 0) else 1
+                tiles_each = 4 // pieces
+                for piece in range(pieces):
+                    first = 512 * half + P * tiles_each * piece
+                    rows = x[first : first + P * tiles_each, 1024 * k_half : 1024 * (k_half + 1)]
+                    nc.sync.dma_start(
+                        out=dest[:, tiles_each * piece : tiles_each * (piece + 1), :], in_=rows.rearrange("(i p) k -> p i k", p=P)
+                    )
             elif kind == "lw":
                 n = item[1]
                 group, g = n // 4, n % 4

@@ -45,7 +45,7 @@ AFTER_GELU = {
     (7, 1): "cs.0 cs.1", (8, 1): "cs.2 cs.3", (10, 3): "cs.4 cs.5", (11, 3): "cs.6 cs.7",
 }
 FIRST_LOAD_PIECES = 2
-CLOCK_KEEPERS = {("xt", 2, 2): 2, ("ot", 0, 0): 2}
+CLOCK_KEEPERS = {("xt", 0, 0): 3, ("mm", 0, 0): 3, ("xt", 2, 2): 2, ("ot", 0, 0): 2}
 FIRST_LATE_CHUNK = 5
 
 
@@ -361,6 +361,8 @@ def tile_modelnew_kernel(tc, x, weight, bn_gamma, bn_beta, bn_mean, bn_var, out_
                 for bank in banks:
                     if ("acc", (s, bank)) not in tiles and (s == FIRST_STEP or bank == bank_of(s, part)[0]):
                         new_tile("acc", (s, bank), 4 // len(banks), [P, 512], F32)
+                for d in range(CLOCK_KEEPERS.get(item, 0)):
+                    nc.tensor.matmul(out=tiles[("acc", (s, 0))][:], lhsT=warm[:, 0:P], rhs=warm[:], start=True, stop=True)
                 for other in range(4):
                     if s == FIRST_STEP:
                         one_pass(s, other, part)

@@ -34,11 +34,10 @@ W_COLS_VECTOR = 288
 CAST_COLS_VECTOR = 1280
 
 VECTOR_HEAD = (
-    "xc.0.0 xc.0.1 xq.0.0 wv.0 xq.1.0 wq.0 xq.0.1 xq.1.1 wv.1 wq.1 xc.0.2 wv.2 xq.0.2 wq.2 xq.1.2 xc.0.3 wv.3 xq.0.3 xq.1.3 wq.3 "
-    "xc.2.0 xq.2.0 xq.3.0 xc.2.1 wv.4 xq.2.1 xc.2.2 xq.3.1 xq.2.2 xc.2.3 wq.4 xq.3.2 xq.2.3 xq.3.3"
+    "xc.0.0 xc.0.1 xq.0.0 wv.0 xq.1.0 wq.0 xq.0.1 xq.1.1 wv.1 wq.1 xc.0.2 wv.2 xq.0.2 wq.2 xq.1.2 wv.3 xq.0.3 xq.1.3 wq.3 xc.2.0 xq.2.0 xq.3.0 xc.2.1 xq.2.1 xc.2.2 xq.3.1 xq.2.2 xc.2.3 xq.3.2 xq.2.3 xq.3.3 wv.4 wv.5 wq.4 wv.6 wq.5 wv.7 wq.6 wq.7"
 )
 SCALAR_HEAD = (
-    "xc.1.0 ws.0 xc.1.1 ws.1 bn ws.2 xc.1.2 ws.3 xc.1.3 xc.3.0 ge.0.0 ge.0.1 ge.0.2 ge.0.3 xc.3.1 ws.4 xc.3.2 xc.3.3 ws.5 ws.6 ws.7"
+    "xc.1.0 ws.0 xc.1.1 ws.1 bn ws.2 xc.1.2 ws.3 xc.0.3 xc.1.3 xc.3.0 ge.0.0 ge.0.1 ge.0.2 ge.0.3 xc.3.1 xc.3.2 xc.3.3 ws.4 ws.5 ws.6 ws.7"
 )
 AFTER_GELU = {
     (1, 2): "ws.8", (2, 0): "ws.9", (2, 2): "ws.10", (2, 3): "ws.11 ws.12", (3, 2): "ws.13", (3, 3): "ws.14 ws.15",
@@ -46,7 +45,7 @@ AFTER_GELU = {
 }
 FIRST_LOAD_PIECES = 2
 CLOCK_KEEPERS = {("xt", 0, 0): 3, ("mm", 0, 0): 3, ("xt", 2, 2): 2, ("ot", 0, 0): 2}
-FIRST_LATE_CHUNK = 5
+FIRST_LATE_CHUNK = 8
 
 
 def parse_items(text):
@@ -87,7 +86,7 @@ def engine_orders():
     vector = parse_items(VECTOR_HEAD)
     finished = []
     for s in steps:
-        trio = list(range(FIRST_LATE_CHUNK + 3 * s, min(FIRST_LATE_CHUNK + 3 * s + 3, 16)))
+        trio = list(range(FIRST_LATE_CHUNK + 3 * (s - 1), min(FIRST_LATE_CHUNK + 3 * s, 16))) if s > 0 else []
         relus = per_tile("re", s)
         vector += [("wv", n) for n in trio[:2]] + [("wq", n) for n in trio[:2]]
         if len(trio) == 3:
@@ -321,7 +320,7 @@ def tile_modelnew_kernel(tc, x, weight, bn_gamma, bn_beta, bn_mean, bn_var, out_
                 dest = new_tile("x4", (pr, g), 1, [P, 256, 4], BF16)
                 dst = dest[:].bitcast(F32).rearrange("p (i r) u -> p i r u", i=2)
                 src = read("turn", ("x", pr, g))[:].rearrange("p i u r -> p i r u")
-                if pr % 2 == 0:
+                if ("xc.%d.%d" % (pr, g)) in VECTOR_HEAD.split():
                     nc.vector.tensor_copy(out=dst, in_=src)
                 else:
                     nc.scalar.copy(out=dst, in_=src)

@@ -275,7 +275,10 @@ def tile_modelnew_kernel(tc, x, weight, bn_gamma, bn_beta, bn_mean, bn_var, out_
                 rows = raw[:, n % 2, :, first:last]
             else:
                 rows = raw[:, :, 512 * (n // 4 - 2) + first : 512 * (n // 4 - 2) + last]
-            copy(out=tiles[("w4", n)][:, first:last, :], in_=rows.rearrange("p j w -> p w j"))
+            copy(
+                out=tiles[("w4", n)][:, first:last, :].rearrange("p (c i) j -> p c j i", i=4),
+                in_=rows.rearrange("p j (c i) -> p c j i", i=4),
+            )
 
         def write_down(item):
             kind = item[0]

@@ -34,7 +34,7 @@ W_COLS_VECTOR = 288
 CAST_COLS_VECTOR = 1280
 
 VECTOR_HEAD = (
-    "xc.0.0 xc.0.1 xq.0.0 wv.0 xq.1.0 wq.0 xq.0.1 xq.1.1 wv.1 wq.1 xc.0.2 wv.2 xq.0.2 wq.2 xq.1.2 wv.3 xq.0.3 xq.1.3 wq.3 xc.2.0 xq.2.0 xq.3.0 xc.2.1 xq.2.1 xc.2.2 xq.3.1 xq.2.2 xc.2.3 xq.3.2 xq.2.3 xq.3.3 wv.4 wv.5 wq.4 wv.6 wq.5 wv.7 wq.6 wq.7"
+    "xc.0.0 xc.0.1 xq.0.0 wv.0 xq.1.0 wq.0 xq.0.1 wv.1 xq.1.1 wq.1 xc.0.2 wv.2 xq.0.2 wq.2 xq.1.2 wv.3 xq.0.3 xq.1.3 wq.3 xc.2.0 xq.3.0 xq.2.0 xc.2.1 xc.2.2 xq.2.1 xq.3.1 xq.2.2 xc.2.3 xq.3.2 xq.2.3 xq.3.3 wv.4 wv.5 wq.4 wv.6 wq.5 wv.7 wq.6 wq.7"
 )
 SCALAR_HEAD = (
     "xc.1.0 ws.0 xc.1.1 ws.1 bn ws.2 xc.1.2 ws.3 xc.0.3 xc.1.3 xc.3.0 ge.0.0 ge.0.1 ge.0.2 ge.0.3 xc.3.1 xc.3.2 xc.3.3 ws.4 ws.5 ws.6 ws.7"

from contextlib import ExitStack

import concourse.mybir as mybir
from concourse.masks import make_identity

TOKENS, K, CHANNELS = 1024, 2048, 2048
EPS = 1e-5
FLOPS = 2 * TOKENS * K * CHANNELS

F32 = mybir.dt.float32
BF16 = mybir.dt.bfloat16
U32 = mybir.dt.uint32
U8 = mybir.dt.uint8
FP8X4 = mybir.dt.float8_e4m3fn_x4
FP8 = mybir.dt.float8_e4m3fn
ACT = mybir.ActivationFunctionType
ALU = mybir.AluOpType
ENGINE = mybir.EngineType

P = 128
PASSES = range(4)
CHANNEL_TILES = range(4)
LAST_GROUP = 3

STEPS = [
    (0, 0, 4), (0, 4, 4), (1, 0, 4), (1, 4, 4), (2, 0, 4), (3, 0, 2),
    (3, 2, 2), (2, 4, 2), (3, 4, 2), (2, 6, 2), (3, 6, 1), (3, 7, 1),
]
FIRST_STEP = 0
OWN_BANK = (0, 10, 11)

SLOTS = {"big": 4, "raw": 4, "x4": 8, "w4": 3, "acc": 4, "turn": 4, "gelu": 8, "fp8": 4}
W_COLS_VECTOR = 288
CAST_COLS_VECTOR = 1280

VECTOR_HEAD = (
    "xc.0.0 xc.0.1 xq.0.0 wv.0 xq.1.0 wq.0 xq.0.1 wv.1 xq.1.1 wq.1 xc.0.2 wv.2 xq.0.2 wq.2 xq.1.2 wv.3 xq.0.3 xq.1.3 wq.3 xc.2.0 xq.3.0 xq.2.0 xc.2.1 xc.2.2 xq.2.1 xq.3.1 xq.2.2 xc.2.3 xq.3.2 xq.2.3 xq.3.3 wv.4 wv.5 wq.4 wv.6 wq.5 wv.7 wq.6 wq.7"
)
SCALAR_HEAD = (
    "xc.1.0 ws.0 xc.1.1 ws.1 bn ws.2 xc.1.2 ws.3 xc.0.3 xc.1.3 xc.3.0 ge.0.0 ge.0.1 ge.0.2 ge.0.3 xc.3.1 xc.3.2 xc.3.3 ws.4 ws.5 ws.6 ws.7"
)
AFTER_GELU = {
    (1, 2): "ws.8", (2, 0): "ws.9", (2, 2): "ws.10", (2, 3): "ws.11 ws.12", (3, 2): "ws.13", (3, 3): "ws.14 ws.15",
    (7, 1): "cs.0 cs.1", (8, 1): "cs.2 cs.3", (10, 3): "cs.4 cs.5", (11, 3): "cs.6 cs.7",
}
FIRST_LOAD_PIECES = 2
CLOCK_KEEPERS = {("xt", 0, 0): 3, ("mm", 0, 0): 3, ("xt", 2, 2): 2, ("ot", 0, 0): 2}
FIRST_LATE_CHUNK = 8


def parse_items(text):
    return [(word.split(".")[0],) + tuple(int(number) for number in word.split(".")[1:]) for word in text.split()]


def tiles_of(s):
    return [STEPS[s][1] + i for i in range(STEPS[s][2])]


def bank_of(s, c):
    width = STEPS[s][2]
    if s in OWN_BANK or width == 4:
        return c, 0
    return (c * width) // 4, ((c * width) % 4) * P


def step_with(group, t):
    s = [i for i in range(len(STEPS)) if STEPS[i][0] == group and t in tiles_of(i)][0]
    return s, t - STEPS[s][1]


def engine_orders():
    per_tile = lambda kind, s: [(kind, s, i) for i in range(STEPS[s][2])]
    steps = range(len(STEPS))

    tensor = [("xt", 0, 0), ("xt", 0, 1), ("xt", 1, 0), ("xt", 1, 1), ("bt",), ("mm", FIRST_STEP, 0)]
    for run in range(2, 8):
        half, g = run // 4, run % 4
        tensor += [("xt", 2 * half, g), ("xt", 2 * half + 1, g)]
        if run <= 4:
            tensor += [("mm", FIRST_STEP, run - 1)]
    tensor += per_tile("ot", FIRST_STEP) + [("mm", 1, c) for c in CHANNEL_TILES]
    for s in steps[2:]:
        tensor += [("mm", s, c) for c in CHANNEL_TILES] + per_tile("ot", s - 1)
    tensor += per_tile("ot", steps[-1])

    vector = parse_items(VECTOR_HEAD)
    finished = []
    for s in steps:
        trio = list(range(FIRST_LATE_CHUNK + 3 * (s - 1), min(FIRST_LATE_CHUNK + 3 * s, 16))) if s > 0 else []
        relus = per_tile("re", s)
        vector += [("wv", n) for n in trio[:2]] + [("wq", n) for n in trio[:2]]
        if len(trio) == 3:
            vector += [("wv", trio[2]), relus[0], ("wq", trio[2])] + relus[1:]
        else:
            vector += relus
        if STEPS[s][0] == LAST_GROUP:
            finished += [s]
            if tiles_of(s)[-1] % 2 == 1:
                vector += [("sc", done) for done in finished] + [("cv", t) for done in finished for t in tiles_of(done)]
                finished = []

    scalar = parse_items(SCALAR_HEAD)
    for s in steps[1:]:
        for c in CHANNEL_TILES:
            scalar += [("ge", s, c)] + parse_items(AFTER_GELU.get((s, c), ""))

    queue = [("lx", 0, 0), ("lw", 0), ("lw", 1), ("lx", 0, 1), ("lw", 2), ("lw", 3), ("lx", 1, 0), ("lx", 1, 1)]
    queue += [("lw", n) for n in range(4, 8)] + [("l2", g) for g in PASSES]
    for s in steps:
        if STEPS[s][0] % 2 == 1:
            queue += per_tile("s0", s)
        if STEPS[s][0] == LAST_GROUP:
            queue += [("s1", t) for t in tiles_of(s)]
    return [tensor, vector, scalar, queue]


def tile_modelnew_kernel(tc, x, weight, bn_gamma, bn_beta, bn_mean, bn_var, out_0, out_1):
    nc = tc.nc
    with ExitStack() as ctx:
        const = ctx.enter_context(tc.tile_pool(name="const", bufs=1))
        keep = ctx.enter_context(tc.tile_pool(name="keep", bufs=1))
        work = ctx.enter_context(tc.tile_pool(name="work", bufs=1))
        psum = ctx.enter_context(tc.psum_pool(name="psum", bufs=4))
        ctx.enter_context(tc.manual_schedule(engines={ENGINE.PE, ENGINE.DVE, ENGINE.Activation}))

        ident = const.tile([P, P], F32, name="ident")
        make_identity(nc, ident[:])
        warm = const.tile([P, 512], BF16, name="warm")
        nc.gpsimd.memset(warm[:], 0.0)
        zero = const.tile([P, 1], F32, name="zero")
        nc.gpsimd.memset(zero[:], 0.0)
        neg_half = const.tile([P, 16], F32, name="neg_half")
        nc.gpsimd.memset(neg_half[:], -0.5)
        vec_bf = const.tile([P, P], BF16, name="vec_bf")
        nc.gpsimd.memset(vec_bf[64:128, :], 0.0)
        for v, vec in enumerate((bn_gamma, bn_beta, bn_mean, bn_var)):
            nc.scalar.dma_start(out=vec_bf[16 * v : 16 * v + 16, :], in_=vec.rearrange("(i p) -> i p", p=P))
        table_warmer = const.tile([P, 1], F32, name="table_warmer")
        nc.scalar.activation(out=table_warmer[:], in_=zero[:], func=ACT.Gelu_apprx_tanh)
        vec_f32 = const.tile([P, P], F32, name="vec_f32")
        nc.gpsimd.tensor_copy(out=vec_f32[:], in_=vec_bf[:])
        bn_cols = const.tile([P, 64], F32, name="bn_cols")
        bn_tmp = const.tile([P, 3, 16], F32, name="bn_tmp")
        bn_scale = const.tile([P, 16], F32, name="bn_scale")
        bn_bias = const.tile([P, 16], F32, name="bn_bias")
        row_max = const.tile([P, 8, 4], F32, name="row_max")
        row_inv = const.tile([P, 8], F32, name="row_inv")
        row_factor = const.tile([P, 8], F32, name="row_factor")

        x_codes = [keep.tile([P, 4, 512], U32, name="x_codes%d" % half, align_bytes=64) for half in range(2)]
        x_scales = [keep.tile([P, 4, 512], U8, name="x_scales%d" % half, align_bytes=64) for half in range(2)]
        w_codes = [keep.tile([P, 4, 512], U32, name="w_codes%d" % group, align_bytes=64) for group in range(4)]
        w_scales = [keep.tile([P, 4, 512], U8, name="w_scales%d" % group, align_bytes=64) for group in range(4)]
        result = keep.tile([P, 8, CHANNELS], F32, name="result")

        tiles = {}
        history = {}
        readers_left = {}

        def has_room(tag, count):
            have = history.setdefault(tag, [])
            for extra in range(count):
                old = len(have) + extra - SLOTS[tag]
                if old >= 0 and (old >= len(have) or readers_left[(tag, have[old])] > 0):
                    return False
            return True

        def new_tile(tag, key, readers, shape, dtype):
            if tag in ("acc", "turn"):
                fresh = psum.tile(shape, dtype, name=tag, tag=tag, bufs=SLOTS[tag])
            else:
                fresh = work.tile(shape, dtype, name=tag, tag=tag, bufs=SLOTS[tag], align_bytes=64)
            tiles[(tag, key)] = fresh
            history.setdefault(tag, []).append(key)
            readers_left[(tag, key)] = readers
            return fresh

        def read(tag, key):
            readers_left[(tag, key)] -= 1
            return tiles[(tag, key)]

        def raw_home(n):
            if n < 4:
                return "raw", n
            if n < 8:
                return "big", ("group 1", (n - 4) // 2)
            return "big", ("groups 2 and 3", n % 4)

        def needs(item):
            kind = item[0]
            if kind == "xt":
                return [("lx", item[1] // 2, item[2] // 2)]
            if kind == "xc":
                return [("xt", item[1], item[2])]
            if kind == "xq":
                return [("xc", item[1], item[2])]
            if kind in ("wv", "ws"):
                return [("lw", item[1])] if item[1] < 8 else [("l2", item[1] % 4)]
            if kind == "wq":
                return [("wv", item[1]), ("ws", item[1])]
            if kind == "bn":
                return [("bt",)]
            if kind == "mm":
                s, part = item[1], item[2]
                passes = [part] if s == FIRST_STEP else PASSES
                pairs = sorted(set(t // 2 for t in tiles_of(s)))
                return [("xq", pr, g) for pr in pairs for g in passes] + [("wq", 4 * STEPS[s][0] + g) for g in passes]
            if kind == "ge":
                s, c = item[1], item[2]
                if s == FIRST_STEP:
                    return [("mm", s, 3), ("bn",)]
                return [("mm", s, cc) for cc in CHANNEL_TILES if bank_of(s, cc)[0] == bank_of(s, c)[0]] + [("bn",)]
            if kind == "ot":
                return [("ge", item[1], c) for c in CHANNEL_TILES]
            if kind == "re":
                return [("ot", item[1], item[2])]
            if kind == "s0":
                return [("re", item[1], item[2]), ("re",) + step_with(STEPS[item[1]][0] - 1, tiles_of(item[1])[item[2]])]
            if kind == "sc":
                return [("re", item[1], i) for i in range(STEPS[item[1]][2])]
            if kind in ("cv", "cs"):
                return [("sc", step_with(LAST_GROUP, item[1])[0])]
            if kind == "s1":
                return [("cv", item[1]), ("cs", item[1])]
            return []

        def new_tiles(item):
            kind = item[0]
            if kind in ("lx", "l2"):
                return "big", 1
            if kind == "lw":
                return raw_home(item[1])[0], 0 if raw_home(item[1]) in tiles else 1
            if kind in ("xt", "ot"):
                return "turn", 1
            if kind == "xc":
                return "x4", 1
            if kind in ("wv", "ws"):
                return "w4", 0 if ("w4", item[1]) in tiles else 1
            if kind == "bt":
                return "acc", 1
            if kind == "mm":
                s, part = item[1], item[2]
                if s == FIRST_STEP:
                    return "acc", 4 if part == 0 else 0
                return "acc", 0 if ("acc", (s, bank_of(s, part)[0])) in tiles else 1
            if kind == "ge":
                return "gelu", 1
            if kind in ("cv", "cs"):
                return "fp8", 0 if ("fp8", item[1]) in tiles else 1
            return "", 0

        def one_pass(s, c, g):
            group, t0, width = STEPS[s]
            half, col, cols = t0 // 4, (t0 % 4) * P, width * P
            bank, first = bank_of(s, c)
            channels = slice(c * P, (c + 1) * P)
            nc.tensor.matmul_mx(
                out=tiles[("acc", (s, bank))][:, first : first + cols],
                lhsT=w_codes[group][:, g, channels].bitcast(FP8X4),
                lhsT_scale=w_scales[group][:, g, channels],
                rhs=x_codes[half][:, g, col : col + cols].bitcast(FP8X4),
                rhs_scale=x_scales[half][:, g, col : col + cols],
                start=(g == 0),
                stop=(g == 3),
            )

        def interleave(n, copy, first, last):
            if ("w4", n) not in tiles:
                new_tile("w4", n, 1, [P, 512, 4], BF16)
            tag, key = raw_home(n)
            raw = read(tag, key)
            if n < 4:
                rows = raw[:, :, first:last]
            elif n < 8:
                rows = raw[:, n % 2, :, first:last]
            else:
                rows = raw[:, :, 512 * (n // 4 - 2) + first : 512 * (n // 4 - 2) + last]
            copy(
                out=tiles[("w4", n)][:, first:last, :].rearrange("p (c i) j -> p c j i", i=4),
                in_=rows.rearrange("p j (c i) -> p c j i", i=4),
            )

        def write_down(item):
            kind = item[0]
            if kind == "lx":
                half, k_half = item[1], item[2]
                dest = new_tile("big", (half, k_half), 4, [P, 4, 1024], BF16)
                pieces = FIRST_LOAD_PIECES if (half, k_half) == (0, 0) else 1
                tiles_each = 4 // pieces
                for piece in range(pieces):
                    first = 512 * half + P * tiles_each * piece
                    rows = x[first : first + P * tiles_each, 1024 * k_half : 1024 * (k_half + 1)]
                    nc.sync.dma_start(
                        out=dest[:, tiles_each * piece : tiles_each * (piece + 1), :], in_=rows.rearrange("(i p) k -> p i k", p=P)
                    )
            elif kind == "lw":
                n = item[1]
                group, g = n // 4, n % 4
                if n < 4:
                    dest = new_tile("raw", n, 2, [P, 4, 512], BF16)[:]
                else:
                    if raw_home(n) not in tiles:
                        new_tile("big", raw_home(n)[1], 4, [P, 2, 4, 512], BF16)
                    dest = tiles[raw_home(n)][:, n % 2, :, :]
                rows = weight[512 * g : 512 * (g + 1), 512 * group : 512 * (group + 1)]
                nc.sync.dma_start(out=dest, in_=rows.rearrange("(p j) w -> p j w", j=4))
            elif kind == "l2":
                g = item[1]
                dest = new_tile("big", ("groups 2 and 3", g), 4, [P, 4, 1024], BF16)
                nc.sync.dma_start(out=dest[:], in_=weight[512 * g : 512 * (g + 1), 1024:2048].rearrange("(p j) w -> p j w", j=4))
            elif kind == "xt":
                pr, g = item[1], item[2]
                bank = new_tile("turn", ("x", pr, g), 1, [P, 2, 2, P], F32)
                for d in range(CLOCK_KEEPERS.get(item, 0)):
                    nc.tensor.matmul(out=bank[:].rearrange("p i u r -> p (i u r)"), lhsT=warm[:, 0:P], rhs=warm[:], start=True, stop=True)
                loaded = read("big", (pr // 2, g // 2))
                for i in range(2):
                    words = loaded[:, 2 * (pr % 2) + i, 512 * (g % 2) : 512 * (g % 2 + 1)].bitcast(F32)
                    for u in range(2):
                        nc.tensor.transpose(bank[:, i, u, :], words[:, u:256:2], ident[:])
            elif kind == "xc":
                pr, g = item[1], item[2]
                dest = new_tile("x4", (pr, g), 1, [P, 256, 4], BF16)
                dst = dest[:].bitcast(F32).rearrange("p (i r) u -> p i r u", i=2)
                src = read("turn", ("x", pr, g))[:].rearrange("p i u r -> p i r u")
                if ("xc.%d.%d" % (pr, g)) in VECTOR_HEAD.split():
                    nc.vector.tensor_copy(out=dst, in_=src)
                else:
                    nc.scalar.copy(out=dst, in_=src)
            elif kind == "xq":
                pr, g = item[1], item[2]
                half, col = pr // 2, (pr % 2) * 256
                nc.vector.quantize_mx(
                    out=x_codes[half][:, g, col : col + 256].bitcast(FP8X4),
                    scales=x_scales[half][:, g, col : col + 256],
                    in_=read("x4", (pr, g))[:].rearrange("p r j -> p (r j)"),
                )
            elif kind == "wv":
                interleave(item[1], nc.vector.tensor_copy, 0, W_COLS_VECTOR)
            elif kind == "ws":
                interleave(item[1], nc.scalar.copy, W_COLS_VECTOR, 512)
            elif kind == "wq":
                group, g = item[1] // 4, item[1] % 4
                nc.vector.quantize_mx(
                    out=w_codes[group][:, g, :].bitcast(FP8X4),
                    scales=w_scales[group][:, g, :],
                    in_=read("w4", item[1])[:].rearrange("p w j -> p (w j)"),
                )
            elif kind == "bt":
                bank = new_tile("acc", "bn", 1, [P, 512], F32)
                nc.tensor.transpose(bank[:, 0:P], vec_f32[:], ident[:])
            elif kind == "bn":
                nc.scalar.copy(out=bn_cols[:], in_=read("acc", "bn")[:, 0:64])
                gamma, beta, mean, var = [bn_cols[:, 16 * v : 16 * v + 16] for v in range(4)]
                nc.gpsimd.tensor_scalar(out=bn_tmp[:, 0, :], in0=var, scalar1=EPS, scalar2=None, op0=ALU.add)
                nc.gpsimd.tensor_tensor(out=bn_tmp[:, 1, :], in0=bn_tmp[:, 0, :], in1=neg_half[:], op=ALU.pow)
                nc.gpsimd.tensor_tensor(out=bn_scale[:], in0=gamma, in1=bn_tmp[:, 1, :], op=ALU.mult)
                nc.gpsimd.tensor_tensor(out=bn_tmp[:, 2, :], in0=mean, in1=bn_scale[:], op=ALU.mult)
                nc.gpsimd.tensor_tensor(out=bn_bias[:], in0=beta, in1=bn_tmp[:, 2, :], op=ALU.subtract)
            elif kind == "mm":
                s, part = item[1], item[2]
                banks = sorted(set(bank_of(s, c)[0] for c in CHANNEL_TILES))
                for bank in banks:
                    if ("acc", (s, bank)) not in tiles and (s == FIRST_STEP or bank == bank_of(s, part)[0]):
                        new_tile("acc", (s, bank), 4 // len(banks), [P, 512], F32)
                for d in range(CLOCK_KEEPERS.get(item, 0)):
                    nc.tensor.matmul(out=tiles[("acc", (s, 0))][:], lhsT=warm[:, 0:P], rhs=warm[:], start=True, stop=True)
                for other in range(4):
                    if s == FIRST_STEP:
                        one_pass(s, other, part)
                    else:
                        one_pass(s, part, other)
            elif kind == "ge":
                s, c = item[1], item[2]
                cols = STEPS[s][2] * P
                bank, first = bank_of(s, c)
                tile_no = 4 * STEPS[s][0] + c
                dest = new_tile("gelu", (s, c), STEPS[s][2], [P, cols], F32)
                nc.scalar.activation(
                    out=dest[:],
                    in_=read("acc", (s, bank))[:, first : first + cols],
                    func=ACT.Gelu_apprx_tanh,
                    bias=bn_bias[:, tile_no : tile_no + 1],
                    scale=bn_scale[:, tile_no : tile_no + 1],
                )
            elif kind == "ot":
                s, i = item[1], item[2]
                bank = new_tile("turn", ("out", s, i), 1, [P, 512], F32)
                for d in range(CLOCK_KEEPERS.get(item, 0)):
                    nc.tensor.matmul(out=bank[:], lhsT=warm[:, 0:P], rhs=warm[:], start=True, stop=True)
                for c in CHANNEL_TILES:
                    nc.tensor.transpose(bank[:, c * P : (c + 1) * P], read("gelu", (s, c))[:, i * P : (i + 1) * P], ident[:])
            elif kind == "re":
                s, i = item[1], item[2]
                group, t = STEPS[s][0], tiles_of(s)[i]
                nc.vector.tensor_scalar(
                    out=result[:, t, 512 * group : 512 * (group + 1)],
                    in0=read("turn", ("out", s, i))[:],
                    scalar1=0.0,
                    scalar2=(row_max[:, t, group - 1 : group] if group > 0 else None),
                    op0=ALU.max,
                    op1=ALU.max,
                    accum_out=row_max[:, t, group : group + 1],
                )
            elif kind == "s0":
                group, t = STEPS[item[1]][0], tiles_of(item[1])[item[2]]
                cols = slice(512 * (group - 1), 512 * (group + 1))
                nc.sync.dma_start(out=out_0[t * P : (t + 1) * P, cols], in_=result[:, t, cols])
            elif kind == "sc":
                ts = slice(tiles_of(item[1])[0], tiles_of(item[1])[-1] + 1)
                nc.vector.reciprocal(out=row_inv[:, ts], in_=row_max[:, ts, LAST_GROUP])
                nc.vector.tensor_scalar(out=row_factor[:, ts], in0=row_inv[:, ts], scalar1=448.0, scalar2=None, op0=ALU.mult)
            elif kind in ("cv", "cs"):
                t = item[1]
                if ("fp8", t) not in tiles:
                    new_tile("fp8", t, 1, [P, CHANNELS], FP8)
                factor = row_factor[:, t : t + 1]
                if kind == "cv":
                    nc.vector.tensor_scalar(
                        out=tiles[("fp8", t)][:, 0:CAST_COLS_VECTOR], in0=result[:, t, 0:CAST_COLS_VECTOR],
                        scalar1=factor, scalar2=None, op0=ALU.mult, saturate=False,
                    )
                else:
                    nc.scalar.activation(
                        out=tiles[("fp8", t)][:, CAST_COLS_VECTOR:CHANNELS], in_=result[:, t, CAST_COLS_VECTOR:CHANNELS],
                        func=ACT.Identity, bias=zero[:, 0:1], scale=factor, saturate=False,
                    )
            elif kind == "s1":
                t = item[1]
                nc.sync.dma_start(out=out_1[t * P : (t + 1) * P, :], in_=read("fp8", t)[:].bitcast(U8))

        def merge_orders(orders):
            written = set()
            heads = [0 for order in orders]
            moved = True
            while moved:
                moved = False
                for e in range(len(orders)):
                    while heads[e] < len(orders[e]):
                        item = orders[e][heads[e]]
                        tag, count = new_tiles(item)
                        if not all(need in written for need in needs(item)) or (count > 0 and not has_room(tag, count)):
                            break
                        write_down(item)
                        written.add(item)
                        heads[e] += 1
                        moved = True
            assert all(heads[e] == len(orders[e]) for e in range(len(orders))), "the orders block each other"

        merge_orders(engine_orders())
